import numpy as np
import ml_dtypes


def mxq(x, axis, fmt="e4m3"):
    dtype, down = {"e4m3": (ml_dtypes.float8_e4m3fn, 7), "e5m2": (ml_dtypes.float8_e5m2, 14)}[fmt]
    v = np.moveaxis(np.asarray(x, np.float32).astype(ml_dtypes.bfloat16).astype(np.float64), axis, -1)
    blocks = v.reshape(v.shape[:-1] + (-1, 32))
    amax = np.abs(blocks).max(-1, keepdims=True)
    byte = np.maximum(np.where(amax > 0, np.frexp(amax)[1] - 1 + 127, 0) - down, 1)
    scale = np.exp2(byte - 127.0)
    codes = (blocks / scale).astype(np.float32).astype(dtype).astype(np.float64)
    return np.moveaxis((codes * scale).reshape(v.shape), -1, axis)


WIDE = False


def mx_kscale(k):
    if not WIDE:
        return np.ones(k)
    levels = np.array([10, -10, 5, -5, 0])
    a = np.random.permutation(np.resize(levels, k // 512 * 4)).reshape(k // 512, 4)
    idx = np.arange(k)
    return np.exp2(a[idx // 512, idx % 128 // 32])


BF16 = ml_dtypes.bfloat16


def bf(x):
    return np.asarray(x, np.float32).astype(BF16)


def f64(x):
    return np.asarray(x).astype(np.float64)


I, H, B = 2048, 2048, 128


def sigmoid(v):
    return 1.0 / (1.0 + np.exp(-v))


def setup_inputs():
    s, t = mx_kscale(I), mx_kscale(H)
    d = {"x": bf(np.random.standard_normal((I, B)) * s[:, None]), "h": bf(np.random.standard_normal((B, H)) * t[None, :])}
    for n in ("w_ii", "w_ig"):
        d[n] = bf(np.random.standard_normal((H, I)) * 0.7 / np.sqrt(I) / s[None, :])
    for n in ("w_hi", "w_hg"):
        d[n] = bf(np.random.standard_normal((H, H)) * 0.7 / np.sqrt(H) / t[None, :])
    for n in ("b_ii", "b_hi", "b_ig", "b_hg"):
        d[n] = bf(np.random.standard_normal((H, 1)) * 0.3)
    return d


def reference(x, h, w_ii, w_ig, w_hi, w_hg, b_ii, b_hi, b_ig, b_hg):
    xq = mxq(f64(x), 0, "e4m3")
    hq = mxq(f64(h).T, 0, "e4m3")
    i = sigmoid((mxq(f64(w_ii), 1, "e4m3") @ xq) + f64(b_ii) + (mxq(f64(w_hi), 1, "e4m3") @ hq) + f64(b_hi))
    g = np.tanh((mxq(f64(w_ig), 1, "e4m3") @ xq) + f64(b_ig) + (mxq(f64(w_hg), 1, "e4m3") @ hq) + f64(b_hg))
    return i * g

@@ -1,0 +1,218 @@
+from contextlib import ExitStack
+
+import concourse.mybir as mybir
+from concourse.masks import make_identity
+
+F32 = mybir.dt.float32
+BF16 = mybir.dt.bfloat16
+U32 = mybir.dt.uint32
+U8 = mybir.dt.uint8
+FP8X4 = mybir.dt.float8_e4m3fn_x4
+ACT = mybir.ActivationFunctionType
+ALU = mybir.AluOpType
+
+P = 128
+K = 2048
+NT = 16
+B = 128
+WORDS = K // 2
+FLOPS = 2 * 4 * 2048 * 2048 * 128
+
+MODE = "B"
+NB = 12
+T_BANKS = 4 if MODE == "B" else 6
+ACC_BANKS = 4 if MODE == "B" else 2
+
+
+def tile_naivelstm_pa_kernel(tc, x, h, w_ii, w_ig, w_hi, w_hg, b_ii, b_hi, b_ig, b_hg, out):
+    nc = tc.nc
+    with ExitStack() as ctx:
+        ctx.enter_context(tc.manual_schedule())
+        const = ctx.enter_context(tc.tile_pool(name="const", bufs=1))
+        rawp = ctx.enter_context(tc.tile_pool(name="rawp", bufs=NB))
+        grpp = ctx.enter_context(tc.tile_pool(name="grpp", bufs=4))
+        codp = ctx.enter_context(tc.tile_pool(name="codp", bufs=8))
+        epip = ctx.enter_context(tc.tile_pool(name="epip", bufs=3))
+        tps = ctx.enter_context(tc.psum_pool(name="tps", bufs=T_BANKS))
+        accp = ctx.enter_context(tc.psum_pool(name="accp", bufs=ACC_BANKS))
+
+        weights = {("i", "x"): w_ii, ("i", "h"): w_hi, ("g", "x"): w_ig, ("g", "h"): w_hg}
+        out_v = out.rearrange("(p t) b -> p t b", t=NT)
+
+        chunks = []
+        for tp in range(NT // 2):
+            for gate in ("i", "g"):
+                for half in ("x", "h"):
+                    chunks.append((gate, half, 2 * tp, 2))
+        last = chunks.pop()
+        chunks.append((last[0], last[1], last[2], 1))
+        chunks.append((last[0], last[1], last[2] + 1, 1))
+        n_chunks = len(chunks)
+
+        raw_tiles = {}
+
+        def load(ci):
+            gate, half, t0, n = chunks[ci]
+            rt = rawp.tile([P, 2 * K], BF16, name="wraw", tag="wraw")
+            src = weights[(gate, half)].rearrange("(p t) k -> p t k", t=NT)[:, t0 : t0 + n, :]
+            nc.sync.dma_start(out=rt[:, : n * K].rearrange("p (t k) -> p t k", t=n), in_=src)
+            raw_tiles[ci] = rt
+
+        ident = const.tile([P, P], F32, name="ident")
+        make_identity(nc, ident[:])
+
+        braw = {}
+        for nm, ap in (("ii", b_ii), ("hi", b_hi), ("ig", b_ig), ("hg", b_hg)):
+            bt = const.tile([P, NT], BF16, name="braw_" + nm)
+            nc.scalar.dma_start(out=bt[:], in_=ap.rearrange("(p t) o -> p (t o)", t=NT))
+            braw[nm] = bt
+
+        hraw = const.tile([P, K], BF16, name="hraw")
+        nc.sync.dma_start(out=hraw[:], in_=h)
+        xraw = const.tile([P, 8, 256], BF16, name="xraw")
+        nc.sync.dma_start(out=xraw[:], in_=x.rearrange("(g u p e) c -> p (g u) (e c)", g=4, u=2, p=P, e=2))
+        for ci in range(NB):
+            load(ci)
+
+        warm = const.tile([P, 1], F32, name="warm")
+        nc.vector.memset(warm[:], 0.0)
+        warm2 = const.tile([P, 1], F32, name="warm2")
+        nc.scalar.activation(out=warm2[:], in_=warm[:], func=ACT.Sigmoid)
+
+        def transposes(src_words):
+            banks = []
+            for b in range(2):
+                tb = tps.tile([P, 4, P], F32, name="tb", tag="tb")
+                for q in range(4):
+                    w0 = (4 * b + q) * P
+                    nc.tensor.transpose(tb[:, q, :], src_words[:, w0 : w0 + P], ident[:])
+                banks.append(tb)
+            return banks
+
+        def copy_bank(eng, grp, b, tb):
+            dst = grp[:].bitcast(F32)[:, 512 * b : 512 * (b + 1)].rearrange("p (g r u) -> p g r u", g=2, u=2)
+            src = tb[:].rearrange("p (g u) r -> p g r u", u=2)
+            if eng == "s":
+                nc.scalar.copy(out=dst, in_=src)
+            else:
+                nc.vector.tensor_copy(out=dst, in_=src)
+
+        def quantise(grp, codes, scl):
+            nc.vector.quantize_mx(out=codes[:].bitcast(FP8X4), scales=scl[:], in_=grp[:])
+
+        hb = transposes(hraw[:].bitcast(F32))
+        hgrp = grpp.tile([P, K], BF16, name="grp", tag="grp", align_bytes=64)
+        copy_bank("s", hgrp, 0, hb[0])
+        copy_bank("v", hgrp, 1, hb[1])
+        xgrp = grpp.tile([P, K], BF16, name="grp", tag="grp", align_bytes=64)
+        nc.vector.tensor_copy(
+            out=xgrp[:].rearrange("p (g c j) -> p g c j", g=4, j=4),
+            in_=xraw[:].rearrange("p a b -> p (a b)").rearrange("p (g j c) -> p g c j", g=4, j=4),
+        )
+        act_codes = {}
+        act_scales = {}
+        for nm, grp in (("h", hgrp), ("x", xgrp)):
+            ac = const.tile([P, 512], U32, name="actc_" + nm, align_bytes=64)
+            asc = const.tile([P, 512], U8, name="acts_" + nm, align_bytes=64)
+            quantise(grp, ac, asc)
+            act_codes[nm] = ac
+            act_scales[nm] = asc
+
+        bias = {}
+        for gate, n0, n1 in (("i", "ii", "hi"), ("g", "ig", "hg")):
+            bs = const.tile([P, NT], F32, name="bias_" + gate)
+            nc.vector.tensor_tensor(out=bs[:], in0=braw[n0][:], in1=braw[n1][:], op=ALU.add)
+            bias[gate] = bs
+
+        mx_plan = {}
+        if MODE == "B":
+            for ci in range(1, n_chunks - 2):
+                mx_plan[ci] = [(ci - 1, j) for j in range(chunks[ci - 1][3])]
+            mx_plan[n_chunks - 1] = [(n_chunks - 3, 0), (n_chunks - 3, 1), (n_chunks - 2, 0), (n_chunks - 1, 0)]
+        else:
+            for ci in range(2, n_chunks - 2, 2):
+                mx_plan[ci] = [(ci - 2, 0), (ci - 1, 0), (ci - 2, 1), (ci - 1, 1)]
+            mx_plan[n_chunks - 1] = [(n_chunks - 3, 0), (n_chunks - 2, 0), (n_chunks - 3, 1), (n_chunks - 1, 0)]
+
+        unit_codes = {}
+        accs = {}
+        gate_out = {}
+
+        def mx_unit(ci, j):
+            gate, half, t0, n = chunks[ci]
+            t = t0 + j
+            if half == "x":
+                accs[(gate, t)] = accp.tile([P, B], F32, name="acc", tag="acc")
+            acc = accs[(gate, t)]
+            codes, scl = unit_codes[(ci, j)]
+            for g in range(4):
+                cols = slice(P * g, P * (g + 1))
+                nc.tensor.matmul_mx(
+                    out=acc[:],
+                    lhsT=codes[:, cols].bitcast(FP8X4),
+                    lhsT_scale=scl[:, cols],
+                    rhs=act_codes[half][:, cols].bitcast(FP8X4),
+                    rhs_scale=act_scales[half][:, cols],
+                    start=(half == "x" and g == 0),
+                    stop=(half == "h" and g == 3),
+                )
+            return (gate, t) if half == "h" else None
+
+        def epilogue(closed):
+            for gate, t in closed:
+                key = (gate, t // 2)
+                if key not in gate_out:
+                    gate_out[key] = epip.tile([P, 2, B], F32, name="go_" + gate, tag="go_" + gate)
+                nc.scalar.activation(
+                    out=gate_out[key][:, t % 2, :],
+                    in_=accs[(gate, t)][:],
+                    func=(ACT.Sigmoid if gate == "i" else ACT.Tanh),
+                    bias=bias[gate][:, t : t + 1],
+                    scale=1.0,
+                )
+            done = [t for gate, t in closed if gate == "g"]
+            if not done:
+                return
+            tp = done[0] // 2
+            osb = epip.tile([P, 2, B], F32, name="osb", tag="osb")
+            if tp == NT // 2 - 1:
+                parts = [(0, 1), (1, 2)]
+            else:
+                parts = [(0, 2)]
+            for lo, hi in parts:
+                nc.vector.tensor_tensor(
+                    out=osb[:, lo:hi, :], in0=gate_out[("i", tp)][:, lo:hi, :], in1=gate_out[("g", tp)][:, lo:hi, :], op=ALU.mult
+                )
+                nc.sync.dma_start(out=out_v[:, 2 * tp + lo : 2 * tp + hi, :], in_=osb[:, lo:hi, :])
+
+        for ci in range(n_chunks):
+            n = chunks[ci][3]
+            words = raw_tiles[ci][:].bitcast(F32)
+            banks = []
+            for j in range(n):
+                banks.append(transposes(words[:, j * WORDS : (j + 1) * WORDS]))
+            if ci + NB < n_chunks:
+                load(ci + NB)
+            grps = []
+            for j in range(n):
+                grps.append(grpp.tile([P, K], BF16, name="grp", tag="grp", align_bytes=64))
+            if n == 2:
+                copy_bank("s", grps[0], 0, banks[0][0])
+                copy_bank("s", grps[0], 1, banks[0][1])
+                copy_bank("s", grps[1], 0, banks[1][0])
+                copy_bank("v", grps[1], 1, banks[1][1])
+            else:
+                copy_bank("s", grps[0], 0, banks[0][0])
+                copy_bank("v", grps[0], 1, banks[0][1])
+            for j in range(n):
+                codes = codp.tile([P, 512], U32, name="codes", tag="codes", align_bytes=64)
+                scl = codp.tile([P, 512], U8, name="scl", tag="scl", align_bytes=64)
+                quantise(grps[j], codes, scl)
+                unit_codes[(ci, j)] = (codes, scl)
+            if ci in mx_plan:
+                closed = []
+                for uc, uj in mx_plan[ci]:
+                    res = mx_unit(uc, uj)
+                    if res is not None:
+                        closed.append(res)
+                epilogue(closed)

@@ -18,7 +18,7 @@ B = 128
 WORDS = K // 2
 FLOPS = 2 * 4 * 2048 * 2048 * 128
 
-MODE = "B"
+MODE = "A"
 NB = 12
 T_BANKS = 4 if MODE == "B" else 6
 ACC_BANKS = 4 if MODE == "B" else 2

@@ -18,10 +18,12 @@ B = 128
 WORDS = K // 2
 FLOPS = 2 * 4 * 2048 * 2048 * 128
 
-MODE = "A"
+RUN = 2
+LAG = 2
 NB = 12
-T_BANKS = 4 if MODE == "B" else 6
-ACC_BANKS = 4 if MODE == "B" else 2
+T_BANKS = 6
+ACC_BANKS = 2
+CODE_BUFS = 2 * (RUN + LAG) + 2
 
 
 def tile_naivelstm_pa_kernel(tc, x, h, w_ii, w_ig, w_hi, w_hg, b_ii, b_hi, b_ig, b_hg, out):
@@ -31,7 +33,7 @@ def tile_naivelstm_pa_kernel(tc, x, h, w_ii, w_ig, w_hi, w_hg, b_ii, b_hi, b_ig,
         const = ctx.enter_context(tc.tile_pool(name="const", bufs=1))
         rawp = ctx.enter_context(tc.tile_pool(name="rawp", bufs=NB))
         grpp = ctx.enter_context(tc.tile_pool(name="grpp", bufs=4))
-        codp = ctx.enter_context(tc.tile_pool(name="codp", bufs=8))
+        codp = ctx.enter_context(tc.tile_pool(name="codp", bufs=CODE_BUFS))
         epip = ctx.enter_context(tc.tile_pool(name="epip", bufs=3))
         tps = ctx.enter_context(tc.psum_pool(name="tps", bufs=T_BANKS))
         accp = ctx.enter_context(tc.psum_pool(name="accp", bufs=ACC_BANKS))
@@ -125,14 +127,16 @@ def tile_naivelstm_pa_kernel(tc, x, h, w_ii, w_ig, w_hi, w_hg, b_ii, b_hi, b_ig,
             bias[gate] = bs
 
         mx_plan = {}
-        if MODE == "B":
-            for ci in range(1, n_chunks - 2):
-                mx_plan[ci] = [(ci - 1, j) for j in range(chunks[ci - 1][3])]
-            mx_plan[n_chunks - 1] = [(n_chunks - 3, 0), (n_chunks - 3, 1), (n_chunks - 2, 0), (n_chunks - 1, 0)]
-        else:
-            for ci in range(2, n_chunks - 2, 2):
-                mx_plan[ci] = [(ci - 2, 0), (ci - 1, 0), (ci - 2, 1), (ci - 1, 1)]
-            mx_plan[n_chunks - 1] = [(n_chunks - 3, 0), (n_chunks - 2, 0), (n_chunks - 3, 1), (n_chunks - 1, 0)]
+        for s in range(NT):
+            if s < NT - 1:
+                units = [(2 * s, 0), (2 * s + 1, 0), (2 * s, 1), (2 * s + 1, 1)]
+            else:
+                units = [(2 * s, 0), (2 * s + 1, 0), (2 * s, 1), (2 * s + 2, 0)]
+            run_last_s = (s // (RUN // 2)) * (RUN // 2) + RUN // 2 - 1
+            place = 2 * run_last_s + 1 + LAG
+            if place >= n_chunks - 2:
+                place = n_chunks - 1
+            mx_plan[place] = mx_plan.get(place, []) + units
 
         unit_codes = {}
         accs = {}
@@ -141,14 +145,14 @@ def tile_naivelstm_pa_kernel(tc, x, h, w_ii, w_ig, w_hi, w_hg, b_ii, b_hi, b_ig,
         def mx_unit(ci, j):
             gate, half, t0, n = chunks[ci]
             t = t0 + j
-            if half == "x":
-                accs[(gate, t)] = accp.tile([P, B], F32, name="acc", tag="acc")
-            acc = accs[(gate, t)]
+            if (gate, t // 2) not in accs:
+                accs[(gate, t // 2)] = accp.tile([P, 2, B], F32, name="acc", tag="acc")
+            acc = accs[(gate, t // 2)][:, t % 2, :]
             codes, scl = unit_codes[(ci, j)]
             for g in range(4):
                 cols = slice(P * g, P * (g + 1))
                 nc.tensor.matmul_mx(
-                    out=acc[:],
+                    out=acc,
                     lhsT=codes[:, cols].bitcast(FP8X4),
                     lhsT_scale=scl[:, cols],
                     rhs=act_codes[half][:, cols].bitcast(FP8X4),
@@ -165,25 +169,22 @@ def tile_naivelstm_pa_kernel(tc, x, h, w_ii, w_ig, w_hi, w_hg, b_ii, b_hi, b_ig,
                     gate_out[key] = epip.tile([P, 2, B], F32, name="go_" + gate, tag="go_" + gate)
                 nc.scalar.activation(
                     out=gate_out[key][:, t % 2, :],
-                    in_=accs[(gate, t)][:],
+                    in_=accs[(gate, t // 2)][:, t % 2, :],
                     func=(ACT.Sigmoid if gate == "i" else ACT.Tanh),
                     bias=bias[gate][:, t : t + 1],
                     scale=1.0,
                 )
-            done = [t for gate, t in closed if gate == "g"]
-            if not done:
-                return
-            tp = done[0] // 2
-            osb = epip.tile([P, 2, B], F32, name="osb", tag="osb")
-            if tp == NT // 2 - 1:
-                parts = [(0, 1), (1, 2)]
-            else:
-                parts = [(0, 2)]
-            for lo, hi in parts:
-                nc.vector.tensor_tensor(
-                    out=osb[:, lo:hi, :], in0=gate_out[("i", tp)][:, lo:hi, :], in1=gate_out[("g", tp)][:, lo:hi, :], op=ALU.mult
-                )
-                nc.sync.dma_start(out=out_v[:, 2 * tp + lo : 2 * tp + hi, :], in_=osb[:, lo:hi, :])
+            for tp in sorted(set([t // 2 for gate, t in closed if gate == "g"])):
+                osb = epip.tile([P, 2, B], F32, name="osb", tag="osb")
+                if tp == NT // 2 - 1:
+                    parts = [(0, 1), (1, 2)]
+                else:
+                    parts = [(0, 2)]
+                for lo, hi in parts:
+                    nc.vector.tensor_tensor(
+                        out=osb[:, lo:hi, :], in0=gate_out[("i", tp)][:, lo:hi, :], in1=gate_out[("g", tp)][:, lo:hi, :], op=ALU.mult
+                    )
+                    nc.sync.dma_start(out=out_v[:, 2 * tp + lo : 2 * tp + hi, :], in_=osb[:, lo:hi, :])
 
         for ci in range(n_chunks):
             n = chunks[ci][3]

@@ -15,15 +15,16 @@ P = 128
 K = 2048
 NT = 16
 B = 128
-WORDS = K // 2
 FLOPS = 2 * 4 * 2048 * 2048 * 128
 
-RUN = 2
-LAG = 2
+PAIRS = 7
+LAG_PASSES = 8
+TAIL_STEPS = 4
 NB = 12
 T_BANKS = 6
 ACC_BANKS = 2
-CODE_BUFS = 2 * (RUN + LAG) + 2
+GRP_BUFS = 6
+CODE_BUFS = 14
 
 
 def tile_naivelstm_pa_kernel(tc, x, h, w_ii, w_ig, w_hi, w_hg, b_ii, b_hi, b_ig, b_hg, out):
@@ -32,33 +33,60 @@ def tile_naivelstm_pa_kernel(tc, x, h, w_ii, w_ig, w_hi, w_hg, b_ii, b_hi, b_ig,
         ctx.enter_context(tc.manual_schedule())
         const = ctx.enter_context(tc.tile_pool(name="const", bufs=1))
         rawp = ctx.enter_context(tc.tile_pool(name="rawp", bufs=NB))
-        grpp = ctx.enter_context(tc.tile_pool(name="grpp", bufs=4))
+        grpp = ctx.enter_context(tc.tile_pool(name="grpp", bufs=GRP_BUFS))
         codp = ctx.enter_context(tc.tile_pool(name="codp", bufs=CODE_BUFS))
-        epip = ctx.enter_context(tc.tile_pool(name="epip", bufs=3))
         tps = ctx.enter_context(tc.psum_pool(name="tps", bufs=T_BANKS))
         accp = ctx.enter_context(tc.psum_pool(name="accp", bufs=ACC_BANKS))
 
         weights = {("i", "x"): w_ii, ("i", "h"): w_hi, ("g", "x"): w_ig, ("g", "h"): w_hg}
         out_v = out.rearrange("(p t) b -> p t b", t=NT)
 
-        chunks = []
-        for tp in range(NT // 2):
-            for gate in ("i", "g"):
-                for half in ("x", "h"):
-                    chunks.append((gate, half, 2 * tp, 2))
-        last = chunks.pop()
-        chunks.append((last[0], last[1], last[2], 1))
-        chunks.append((last[0], last[1], last[2] + 1, 1))
-        n_chunks = len(chunks)
+        stream = []
+        for pair in range(PAIRS):
+            for gate in "ig":
+                for half in "xh":
+                    stream.append((gate, half, 2 * pair, 2, 0, 4))
+        for gate in "ig":
+            for t in range(2 * PAIRS, NT):
+                for half in "xh":
+                    stream.append((gate, half, t, 1, 0, 4))
+        stream.pop()
+        stream.append(("g", "h", NT - 1, 1, 0, 2))
+        stream.append(("g", "h", NT - 1, 1, 2, 2))
+        n_steps = len(stream)
 
         raw_tiles = {}
 
         def load(ci):
-            gate, half, t0, n = chunks[ci]
+            gate, half, t0, n, g0, ng = stream[ci]
             rt = rawp.tile([P, 2 * K], BF16, name="wraw", tag="wraw")
-            src = weights[(gate, half)].rearrange("(p t) k -> p t k", t=NT)[:, t0 : t0 + n, :]
-            nc.sync.dma_start(out=rt[:, : n * K].rearrange("p (t k) -> p t k", t=n), in_=src)
+            src = weights[(gate, half)].rearrange("(p t) k -> p t k", t=NT)[:, t0 : t0 + n, 512 * g0 : 512 * (g0 + ng)]
+            nc.sync.dma_start(out=rt[:, : n * ng * 512].rearrange("p (t k) -> p t k", t=n), in_=src)
             raw_tiles[ci] = rt
+
+        group_units = {}
+        for ci in range(n_steps):
+            gate, half, t0, n, g0, ng = stream[ci]
+            for j in range(n):
+                group_units[(gate, t0 + j)] = group_units.get((gate, t0 + j), []) + [(ci, j)]
+        sets = []
+        for pair in range(NT // 2):
+            for gate in "ig":
+                if pair < PAIRS:
+                    sets.append([(gate, 2 * pair), (gate, 2 * pair + 1)])
+        for gate in "ig":
+            for t in range(2 * PAIRS, NT):
+                sets.append([(gate, t)])
+        runs = {}
+        for st in sets:
+            place = max([group_units[grp][-1][0] for grp in st])
+            ahead = 0
+            while place < n_steps - 1 and ahead < LAG_PASSES:
+                place += 1
+                ahead += stream[place][3] * stream[place][5]
+            if place >= n_steps - TAIL_STEPS:
+                place = n_steps - 1
+            runs[place] = runs.get(place, []) + [st]
 
         ident = const.tile([P, P], F32, name="ident")
         make_identity(nc, ident[:])
@@ -81,9 +109,14 @@ def tile_naivelstm_pa_kernel(tc, x, h, w_ii, w_ig, w_hi, w_hg, b_ii, b_hi, b_ig,
         warm2 = const.tile([P, 1], F32, name="warm2")
         nc.scalar.activation(out=warm2[:], in_=warm[:], func=ACT.Sigmoid)
 
-        def transposes(src_words):
+        gate_out = {}
+        for gate in "ig":
+            gate_out[gate] = const.tile([P, NT, B], F32, name="gate_" + gate)
+        osb = const.tile([P, NT, B], F32, name="osb")
+
+        def transposes(src_words, ng):
             banks = []
-            for b in range(2):
+            for b in range(ng // 2):
                 tb = tps.tile([P, 4, P], F32, name="tb", tag="tb")
                 for q in range(4):
                     w0 = (4 * b + q) * P
@@ -99,10 +132,12 @@ def tile_naivelstm_pa_kernel(tc, x, h, w_ii, w_ig, w_hi, w_hg, b_ii, b_hi, b_ig,
             else:
                 nc.vector.tensor_copy(out=dst, in_=src)
 
-        def quantise(grp, codes, scl):
-            nc.vector.quantize_mx(out=codes[:].bitcast(FP8X4), scales=scl[:], in_=grp[:])
+        def quantise(grp, codes, scl, ng):
+            nc.vector.quantize_mx(
+                out=codes[:, : P * ng].bitcast(FP8X4), scales=scl[:, : P * ng], in_=grp[:, : 512 * ng]
+            )
 
-        hb = transposes(hraw[:].bitcast(F32))
+        hb = transposes(hraw[:].bitcast(F32), 4)
         hgrp = grpp.tile([P, K], BF16, name="grp", tag="grp", align_bytes=64)
         copy_bank("s", hgrp, 0, hb[0])
         copy_bank("v", hgrp, 1, hb[1])
@@ -116,7 +151,7 @@ def tile_naivelstm_pa_kernel(tc, x, h, w_ii, w_ig, w_hi, w_hg, b_ii, b_hi, b_ig,
         for nm, grp in (("h", hgrp), ("x", xgrp)):
             ac = const.tile([P, 512], U32, name="actc_" + nm, align_bytes=64)
             asc = const.tile([P, 512], U8, name="acts_" + nm, align_bytes=64)
-            quantise(grp, ac, asc)
+            quantise(grp, ac, asc, 4)
             act_codes[nm] = ac
             act_scales[nm] = asc
 
@@ -126,94 +161,68 @@ def tile_naivelstm_pa_kernel(tc, x, h, w_ii, w_ig, w_hi, w_hg, b_ii, b_hi, b_ig,
             nc.vector.tensor_tensor(out=bs[:], in0=braw[n0][:], in1=braw[n1][:], op=ALU.add)
             bias[gate] = bs
 
-        mx_plan = {}
-        for s in range(NT):
-            if s < NT - 1:
-                units = [(2 * s, 0), (2 * s + 1, 0), (2 * s, 1), (2 * s + 1, 1)]
-            else:
-                units = [(2 * s, 0), (2 * s + 1, 0), (2 * s, 1), (2 * s + 2, 0)]
-            run_last_s = (s // (RUN // 2)) * (RUN // 2) + RUN // 2 - 1
-            place = 2 * run_last_s + 1 + LAG
-            if place >= n_chunks - 2:
-                place = n_chunks - 1
-            mx_plan[place] = mx_plan.get(place, []) + units
-
         unit_codes = {}
-        accs = {}
-        gate_out = {}
 
-        def mx_unit(ci, j):
-            gate, half, t0, n = chunks[ci]
-            t = t0 + j
-            if (gate, t // 2) not in accs:
-                accs[(gate, t // 2)] = accp.tile([P, 2, B], F32, name="acc", tag="acc")
-            acc = accs[(gate, t // 2)][:, t % 2, :]
-            codes, scl = unit_codes[(ci, j)]
-            for g in range(4):
-                cols = slice(P * g, P * (g + 1))
-                nc.tensor.matmul_mx(
-                    out=acc,
-                    lhsT=codes[:, cols].bitcast(FP8X4),
-                    lhsT_scale=scl[:, cols],
-                    rhs=act_codes[half][:, cols].bitcast(FP8X4),
-                    rhs_scale=act_scales[half][:, cols],
-                    start=(half == "x" and g == 0),
-                    stop=(half == "h" and g == 3),
-                )
-            return (gate, t) if half == "h" else None
-
-        def epilogue(closed):
-            for gate, t in closed:
-                key = (gate, t // 2)
-                if key not in gate_out:
-                    gate_out[key] = epip.tile([P, 2, B], F32, name="go_" + gate, tag="go_" + gate)
+        def mx_set(st):
+            acc = accp.tile([P, 2, B], F32, name="acc", tag="acc")
+            for si, grp in enumerate(st):
+                passes = []
+                for ci, j in group_units[grp]:
+                    for gl in range(stream[ci][5]):
+                        passes.append((ci, j, gl))
+                for pi, (ci, j, gl) in enumerate(passes):
+                    half = stream[ci][1]
+                    g = stream[ci][4] + gl
+                    codes, scl = unit_codes[(ci, j)]
+                    nc.tensor.matmul_mx(
+                        out=acc[:, si, :],
+                        lhsT=codes[:, P * gl : P * (gl + 1)].bitcast(FP8X4),
+                        lhsT_scale=scl[:, P * gl : P * (gl + 1)],
+                        rhs=act_codes[half][:, P * g : P * (g + 1)].bitcast(FP8X4),
+                        rhs_scale=act_scales[half][:, P * g : P * (g + 1)],
+                        start=(pi == 0),
+                        stop=(pi == len(passes) - 1),
+                    )
+            gate = st[0][0]
+            for si, (gt, t) in enumerate(st):
                 nc.scalar.activation(
-                    out=gate_out[key][:, t % 2, :],
-                    in_=accs[(gate, t // 2)][:, t % 2, :],
+                    out=gate_out[gate][:, t, :],
+                    in_=acc[:, si, :],
                     func=(ACT.Sigmoid if gate == "i" else ACT.Tanh),
                     bias=bias[gate][:, t : t + 1],
                     scale=1.0,
                 )
-            for tp in sorted(set([t // 2 for gate, t in closed if gate == "g"])):
-                osb = epip.tile([P, 2, B], F32, name="osb", tag="osb")
-                if tp == NT // 2 - 1:
-                    parts = [(0, 1), (1, 2)]
-                else:
-                    parts = [(0, 2)]
-                for lo, hi in parts:
-                    nc.vector.tensor_tensor(
-                        out=osb[:, lo:hi, :], in0=gate_out[("i", tp)][:, lo:hi, :], in1=gate_out[("g", tp)][:, lo:hi, :], op=ALU.mult
-                    )
-                    nc.sync.dma_start(out=out_v[:, 2 * tp + lo : 2 * tp + hi, :], in_=osb[:, lo:hi, :])
+            if gate == "g":
+                lo = st[0][1]
+                hi = st[-1][1] + 1
+                nc.vector.tensor_tensor(
+                    out=osb[:, lo:hi, :], in0=gate_out["i"][:, lo:hi, :], in1=gate_out["g"][:, lo:hi, :], op=ALU.mult
+                )
+                if hi == 2 * PAIRS:
+                    nc.sync.dma_start(out=out_v[:, 0:hi, :], in_=osb[:, 0:hi, :])
+                elif hi > 2 * PAIRS:
+                    nc.sync.dma_start(out=out_v[:, lo:hi, :], in_=osb[:, lo:hi, :])
 
-        for ci in range(n_chunks):
-            n = chunks[ci][3]
+        bank_count = 0
+        for ci in range(n_steps):
+            gate, half, t0, n, g0, ng = stream[ci]
             words = raw_tiles[ci][:].bitcast(F32)
             banks = []
             for j in range(n):
-                banks.append(transposes(words[:, j * WORDS : (j + 1) * WORDS]))
-            if ci + NB < n_chunks:
+                banks.append(transposes(words[:, j * 256 * ng : (j + 1) * 256 * ng], ng))
+            if ci + NB < n_steps:
                 load(ci + NB)
             grps = []
             for j in range(n):
-                grps.append(grpp.tile([P, K], BF16, name="grp", tag="grp", align_bytes=64))
-            if n == 2:
-                copy_bank("s", grps[0], 0, banks[0][0])
-                copy_bank("s", grps[0], 1, banks[0][1])
-                copy_bank("s", grps[1], 0, banks[1][0])
-                copy_bank("v", grps[1], 1, banks[1][1])
-            else:
-                copy_bank("s", grps[0], 0, banks[0][0])
-                copy_bank("v", grps[0], 1, banks[0][1])
+                grp = grpp.tile([P, K], BF16, name="grp", tag="grp", align_bytes=64)
+                grps.append(grp)
+                for b, tb in enumerate(banks[j]):
+                    bank_count += 1
+                    copy_bank("v" if (ng == 4 and bank_count % 4 == 0) else "s", grp, b, tb)
             for j in range(n):
                 codes = codp.tile([P, 512], U32, name="codes", tag="codes", align_bytes=64)
                 scl = codp.tile([P, 512], U8, name="scl", tag="scl", align_bytes=64)
-                quantise(grps[j], codes, scl)
+                quantise(grps[j], codes, scl, ng)
                 unit_codes[(ci, j)] = (codes, scl)
-            if ci in mx_plan:
-                closed = []
-                for uc, uj in mx_plan[ci]:
-                    res = mx_unit(uc, uj)
-                    if res is not None:
-                        closed.append(res)
-                epilogue(closed)
+            for st in runs.get(ci, []):
+                mx_set(st)

@@ -20,6 +20,7 @@ FLOPS = 2 * 4 * 2048 * 2048 * 128
 PAIRS = 7
 LAG_PASSES = 8
 TAIL_STEPS = 4
+V_SHARE = 5
 NB = 12
 T_BANKS = 6
 ACC_BANKS = 2
@@ -218,7 +219,8 @@ def tile_naivelstm_pa_kernel(tc, x, h, w_ii, w_ig, w_hi, w_hg, b_ii, b_hi, b_ig,
                 grps.append(grp)
                 for b, tb in enumerate(banks[j]):
                     bank_count += 1
-                    copy_bank("v" if (ng == 4 and bank_count % 4 == 0) else "s", grp, b, tb)
+                    on_vector = ng == 4 and (V_SHARE * bank_count) // 16 > (V_SHARE * (bank_count - 1)) // 16
+                    copy_bank("v" if on_vector else "s", grp, b, tb)
             for j in range(n):
                 codes = codp.tile([P, 512], U32, name="codes", tag="codes", align_bytes=64)
                 scl = codp.tile([P, 512], U8, name="scl", tag="scl", align_bytes=64)

@@ -20,7 +20,6 @@ FLOPS = 2 * 4 * 2048 * 2048 * 128
 PAIRS = 7
 LAG_PASSES = 8
 TAIL_STEPS = 4
-V_SHARE = 5
 NB = 12
 T_BANKS = 6
 ACC_BANKS = 2
@@ -74,7 +73,8 @@ def tile_naivelstm_pa_kernel(tc, x, h, w_ii, w_ig, w_hi, w_hg, b_ii, b_hi, b_ig,
         for pair in range(NT // 2):
             for gate in "ig":
                 if pair < PAIRS:
-                    sets.append([(gate, 2 * pair), (gate, 2 * pair + 1)])
+                    sets.append([(gate, 2 * pair)])
+                    sets.append([(gate, 2 * pair + 1)])
         for gate in "ig":
             for t in range(2 * PAIRS, NT):
                 sets.append([(gate, t)])
@@ -85,6 +85,8 @@ def tile_naivelstm_pa_kernel(tc, x, h, w_ii, w_ig, w_hi, w_hg, b_ii, b_hi, b_ig,
             while place < n_steps - 1 and ahead < LAG_PASSES:
                 place += 1
                 ahead += stream[place][3] * stream[place][5]
+            if st[0][1] < 2 * PAIRS and st[0][1] % 2 == 1:
+                place += 1
             if place >= n_steps - TAIL_STEPS:
                 place = n_steps - 1
             runs[place] = runs.get(place, []) + [st]
@@ -193,9 +195,9 @@ def tile_naivelstm_pa_kernel(tc, x, h, w_ii, w_ig, w_hi, w_hg, b_ii, b_hi, b_ig,
                     bias=bias[gate][:, t : t + 1],
                     scale=1.0,
                 )
-            if gate == "g":
-                lo = st[0][1]
-                hi = st[-1][1] + 1
+            hi = st[-1][1] + 1
+            lo = hi - 1 if hi > 2 * PAIRS else hi - 2
+            if gate == "g" and (hi > 2 * PAIRS or hi % 2 == 0):
                 nc.vector.tensor_tensor(
                     out=osb[:, lo:hi, :], in0=gate_out["i"][:, lo:hi, :], in1=gate_out["g"][:, lo:hi, :], op=ALU.mult
                 )
@@ -219,8 +221,7 @@ def tile_naivelstm_pa_kernel(tc, x, h, w_ii, w_ig, w_hi, w_hg, b_ii, b_hi, b_ig,
                 grps.append(grp)
                 for b, tb in enumerate(banks[j]):
                     bank_count += 1
-                    on_vector = ng == 4 and (V_SHARE * bank_count) // 16 > (V_SHARE * (bank_count - 1)) // 16
-                    copy_bank("v" if on_vector else "s", grp, b, tb)
+                    copy_bank("v" if (ng == 4 and bank_count % 4 == 0) else "s", grp, b, tb)
             for j in range(n):
                 codes = codp.tile([P, 512], U32, name="codes", tag="codes", align_bytes=64)
                 scl = codp.tile([P, 512], U8, name="scl", tag="scl", align_bytes=64)

@@ -20,6 +20,7 @@ FLOPS = 2 * 4 * 2048 * 2048 * 128
 PAIRS = 7
 LAG_PASSES = 8
 TAIL_STEPS = 4
+HEAD_STEPS = 2
 NB = 12
 T_BANKS = 6
 ACC_BANKS = 2
@@ -42,10 +43,14 @@ def tile_naivelstm_pa_kernel(tc, x, h, w_ii, w_ig, w_hi, w_hg, b_ii, b_hi, b_ig,
         out_v = out.rearrange("(p t) b -> p t b", t=NT)
 
         stream = []
+        for t in range(2):
+            for half in "xh":
+                stream.append(("i", half, t, 1, 0, 4))
         for pair in range(PAIRS):
             for gate in "ig":
                 for half in "xh":
-                    stream.append((gate, half, 2 * pair, 2, 0, 4))
+                    if pair > 0 or gate == "g":
+                        stream.append((gate, half, 2 * pair, 2, 0, 4))
         for gate in "ig":
             for t in range(2 * PAIRS, NT):
                 for half in "xh":
@@ -85,7 +90,7 @@ def tile_naivelstm_pa_kernel(tc, x, h, w_ii, w_ig, w_hi, w_hg, b_ii, b_hi, b_ig,
             while place < n_steps - 1 and ahead < LAG_PASSES:
                 place += 1
                 ahead += stream[place][3] * stream[place][5]
-            if st[0][1] < 2 * PAIRS and st[0][1] % 2 == 1:
+            if stream[group_units[st[0]][-1][0]][3] == 2 and st[0][1] % 2 == 1:
                 place += 1
             if place >= n_steps - TAIL_STEPS:
                 place = n_steps - 1
@@ -100,11 +105,13 @@ def tile_naivelstm_pa_kernel(tc, x, h, w_ii, w_ig, w_hi, w_hg, b_ii, b_hi, b_ig,
             nc.scalar.dma_start(out=bt[:], in_=ap.rearrange("(p t) o -> p (t o)", t=NT))
             braw[nm] = bt
 
+        for ci in range(HEAD_STEPS):
+            load(ci)
         hraw = const.tile([P, K], BF16, name="hraw")
         nc.sync.dma_start(out=hraw[:], in_=h)
         xraw = const.tile([P, 8, 256], BF16, name="xraw")
         nc.sync.dma_start(out=xraw[:], in_=x.rearrange("(g u p e) c -> p (g u) (e c)", g=4, u=2, p=P, e=2))
-        for ci in range(NB):
+        for ci in range(HEAD_STEPS, NB):
             load(ci)
 
         warm = const.tile([P, 1], F32, name="warm")
@@ -140,29 +147,31 @@ def tile_naivelstm_pa_kernel(tc, x, h, w_ii, w_ig, w_hi, w_hg, b_ii, b_hi, b_ig,
                 out=codes[:, : P * ng].bitcast(FP8X4), scales=scl[:, : P * ng], in_=grp[:, : 512 * ng]
             )
 
-        hb = transposes(hraw[:].bitcast(F32), 4)
-        hgrp = grpp.tile([P, K], BF16, name="grp", tag="grp", align_bytes=64)
-        copy_bank("s", hgrp, 0, hb[0])
-        copy_bank("v", hgrp, 1, hb[1])
-        xgrp = grpp.tile([P, K], BF16, name="grp", tag="grp", align_bytes=64)
-        nc.vector.tensor_copy(
-            out=xgrp[:].rearrange("p (g c j) -> p g c j", g=4, j=4),
-            in_=xraw[:].rearrange("p a b -> p (a b)").rearrange("p (g j c) -> p g c j", g=4, j=4),
-        )
         act_codes = {}
         act_scales = {}
-        for nm, grp in (("h", hgrp), ("x", xgrp)):
-            ac = const.tile([P, 512], U32, name="actc_" + nm, align_bytes=64)
-            asc = const.tile([P, 512], U8, name="acts_" + nm, align_bytes=64)
-            quantise(grp, ac, asc, 4)
-            act_codes[nm] = ac
-            act_scales[nm] = asc
-
         bias = {}
-        for gate, n0, n1 in (("i", "ii", "hi"), ("g", "ig", "hg")):
-            bs = const.tile([P, NT], F32, name="bias_" + gate)
-            nc.vector.tensor_tensor(out=bs[:], in0=braw[n0][:], in1=braw[n1][:], op=ALU.add)
-            bias[gate] = bs
+
+        def prepare_activations():
+            hb = transposes(hraw[:].bitcast(F32), 4)
+            hgrp = grpp.tile([P, K], BF16, name="grp", tag="grp", align_bytes=64)
+            copy_bank("s", hgrp, 0, hb[0])
+            copy_bank("v", hgrp, 1, hb[1])
+            xgrp = grpp.tile([P, K], BF16, name="grp", tag="grp", align_bytes=64)
+            nc.vector.tensor_copy(
+                out=xgrp[:].rearrange("p (g c j) -> p g c j", g=4, j=4),
+                in_=xraw[:].rearrange("p a b -> p (a b)").rearrange("p (g j c) -> p g c j", g=4, j=4),
+            )
+            for nm, grp in (("h", hgrp), ("x", xgrp)):
+                ac = const.tile([P, 512], U32, name="actc_" + nm, align_bytes=64)
+                asc = const.tile([P, 512], U8, name="acts_" + nm, align_bytes=64)
+                quantise(grp, ac, asc, 4)
+                act_codes[nm] = ac
+                act_scales[nm] = asc
+
+            for gate, n0, n1 in (("i", "ii", "hi"), ("g", "ig", "hg")):
+                bs = const.tile([P, NT], F32, name="bias_" + gate)
+                nc.vector.tensor_tensor(out=bs[:], in0=braw[n0][:], in1=braw[n1][:], op=ALU.add)
+                bias[gate] = bs
 
         unit_codes = {}
 
@@ -208,6 +217,8 @@ def tile_naivelstm_pa_kernel(tc, x, h, w_ii, w_ig, w_hi, w_hg, b_ii, b_hi, b_ig,
 
         bank_count = 0
         for ci in range(n_steps):
+            if ci == HEAD_STEPS:
+                prepare_activations()
             gate, half, t0, n, g0, ng = stream[ci]
             words = raw_tiles[ci][:].bitcast(F32)
             banks = []

from contextlib import ExitStack

import concourse.mybir as mybir
from concourse.masks import make_identity

F32 = mybir.dt.float32
BF16 = mybir.dt.bfloat16
U32 = mybir.dt.uint32
U8 = mybir.dt.uint8
FP8X4 = mybir.dt.float8_e4m3fn_x4
ACT = mybir.ActivationFunctionType
ALU = mybir.AluOpType

P = 128
K = 2048
NT = 16
B = 128
FLOPS = 2 * 4 * 2048 * 2048 * 128

PAIRS = 7
LAG_PASSES = 8
TAIL_STEPS = 4
HEAD_STEPS = 2
NB = 12
T_BANKS = 6
ACC_BANKS = 2
GRP_BUFS = 6
CODE_BUFS = 14


def tile_naivelstm_pa_kernel(tc, x, h, w_ii, w_ig, w_hi, w_hg, b_ii, b_hi, b_ig, b_hg, out):
    nc = tc.nc
    with ExitStack() as ctx:
        ctx.enter_context(tc.manual_schedule())
        const = ctx.enter_context(tc.tile_pool(name="const", bufs=1))
        rawp = ctx.enter_context(tc.tile_pool(name="rawp", bufs=NB))
        grpp = ctx.enter_context(tc.tile_pool(name="grpp", bufs=GRP_BUFS))
        codp = ctx.enter_context(tc.tile_pool(name="codp", bufs=CODE_BUFS))
        tps = ctx.enter_context(tc.psum_pool(name="tps", bufs=T_BANKS))
        accp = ctx.enter_context(tc.psum_pool(name="accp", bufs=ACC_BANKS))

        weights = {("i", "x"): w_ii, ("i", "h"): w_hi, ("g", "x"): w_ig, ("g", "h"): w_hg}
        out_v = out.rearrange("(p t) b -> p t b", t=NT)

        stream = []
        for t in range(2):
            for half in "xh":
                stream.append(("i", half, t, 1, 0, 4))
        for pair in range(PAIRS):
            for gate in "ig":
                for half in "xh":
                    if pair > 0 or gate == "g":
                        stream.append((gate, half, 2 * pair, 2, 0, 4))
        for gate in "ig":
            for t in range(2 * PAIRS, NT):
                for half in "xh":
                    stream.append((gate, half, t, 1, 0, 4))
        stream.pop()
        stream.append(("g", "h", NT - 1, 1, 0, 2))
        stream.append(("g", "h", NT - 1, 1, 2, 2))
        n_steps = len(stream)

        raw_tiles = {}

        def load(ci):
            gate, half, t0, n, g0, ng = stream[ci]
            rt = rawp.tile([P, 2 * K], BF16, name="wraw", tag="wraw")
            src = weights[(gate, half)].rearrange("(p t) k -> p t k", t=NT)[:, t0 : t0 + n, 512 * g0 : 512 * (g0 + ng)]
            nc.sync.dma_start(out=rt[:, : n * ng * 512].rearrange("p (t k) -> p t k", t=n), in_=src)
            raw_tiles[ci] = rt

        group_units = {}
        for ci in range(n_steps):
            gate, half, t0, n, g0, ng = stream[ci]
            for j in range(n):
                group_units[(gate, t0 + j)] = group_units.get((gate, t0 + j), []) + [(ci, j)]
        sets = []
        for pair in range(NT // 2):
            for gate in "ig":
                if pair < PAIRS:
                    sets.append([(gate, 2 * pair)])
                    sets.append([(gate, 2 * pair + 1)])
        for gate in "ig":
            for t in range(2 * PAIRS, NT):
                sets.append([(gate, t)])
        runs = {}
        for st in sets:
            place = max([group_units[grp][-1][0] for grp in st])
            ahead = 0
            while place < n_steps - 1 and ahead < LAG_PASSES:
                place += 1
                ahead += stream[place][3] * stream[place][5]
            if stream[group_units[st[0]][-1][0]][3] == 2 and st[0][1] % 2 == 1:
                place += 1
            if place >= n_steps - TAIL_STEPS:
                place = n_steps - 1
            runs[place] = runs.get(place, []) + [st]

        ident = const.tile([P, P], F32, name="ident")
        make_identity(nc, ident[:])

        braw = {}
        for nm, ap in (("ii", b_ii), ("hi", b_hi), ("ig", b_ig), ("hg", b_hg)):
            bt = const.tile([P, NT], BF16, name="braw_" + nm)
            nc.scalar.dma_start(out=bt[:], in_=ap.rearrange("(p t) o -> p (t o)", t=NT))
            braw[nm] = bt

        for ci in range(HEAD_STEPS):
            load(ci)
        hraw = const.tile([P, K], BF16, name="hraw")
        nc.sync.dma_start(out=hraw[:], in_=h)
        xraw = const.tile([P, 8, 256], BF16, name="xraw")
        nc.sync.dma_start(out=xraw[:], in_=x.rearrange("(g u p e) c -> p (g u) (e c)", g=4, u=2, p=P, e=2))
        for ci in range(HEAD_STEPS, NB):
            load(ci)

        warm = const.tile([P, 1], F32, name="warm")
        nc.vector.memset(warm[:], 0.0)
        warm2 = const.tile([P, 1], F32, name="warm2")
        nc.scalar.activation(out=warm2[:], in_=warm[:], func=ACT.Sigmoid)

        gate_out = {}
        for gate in "ig":
            gate_out[gate] = const.tile([P, NT, B], F32, name="gate_" + gate)
        osb = const.tile([P, NT, B], F32, name="osb")

        def transposes(src_words, ng):
            banks = []
            for b in range(ng // 2):
                tb = tps.tile([P, 4, P], F32, name="tb", tag="tb")
                for q in range(4):
                    w0 = (4 * b + q) * P
                    nc.tensor.transpose(tb[:, q, :], src_words[:, w0 : w0 + P], ident[:])
                banks.append(tb)
            return banks

        def copy_bank(eng, grp, b, tb):
            dst = grp[:].bitcast(F32)[:, 512 * b : 512 * (b + 1)].rearrange("p (g r u) -> p g r u", g=2, u=2)
            src = tb[:].rearrange("p (g u) r -> p g r u", u=2)
            if eng == "s":
                nc.scalar.copy(out=dst, in_=src)
            else:
                nc.vector.tensor_copy(out=dst, in_=src)

        def quantise(grp, codes, scl, ng):
            nc.vector.quantize_mx(
                out=codes[:, : P * ng].bitcast(FP8X4), scales=scl[:, : P * ng], in_=grp[:, : 512 * ng]
            )

        act_codes = {}
        act_scales = {}
        bias = {}

        def prepare_activations():
            hb = transposes(hraw[:].bitcast(F32), 4)
            hgrp = grpp.tile([P, K], BF16, name="grp", tag="grp", align_bytes=64)
            copy_bank("s", hgrp, 0, hb[0])
            copy_bank("v", hgrp, 1, hb[1])
            xgrp = grpp.tile([P, K], BF16, name="grp", tag="grp", align_bytes=64)
            nc.vector.tensor_copy(
                out=xgrp[:].rearrange("p (g c j) -> p g c j", g=4, j=4),
                in_=xraw[:].rearrange("p a b -> p (a b)").rearrange("p (g j c) -> p g c j", g=4, j=4),
            )
            for nm, grp in (("h", hgrp), ("x", xgrp)):
                ac = const.tile([P, 512], U32, name="actc_" + nm, align_bytes=64)
                asc = const.tile([P, 512], U8, name="acts_" + nm, align_bytes=64)
                quantise(grp, ac, asc, 4)
                act_codes[nm] = ac
                act_scales[nm] = asc

            for gate, n0, n1 in (("i", "ii", "hi"), ("g", "ig", "hg")):
                bs = const.tile([P, NT], F32, name="bias_" + gate)
                nc.vector.tensor_tensor(out=bs[:], in0=braw[n0][:], in1=braw[n1][:], op=ALU.add)
                bias[gate] = bs

        unit_codes = {}

        def mx_set(st):
            acc = accp.tile([P, 2, B], F32, name="acc", tag="acc")
            for si, grp in enumerate(st):
                passes = []
                for ci, j in group_units[grp]:
                    for gl in range(stream[ci][5]):
                        passes.append((ci, j, gl))
                for pi, (ci, j, gl) in enumerate(passes):
                    half = stream[ci][1]
                    g = stream[ci][4] + gl
                    codes, scl = unit_codes[(ci, j)]
                    nc.tensor.matmul_mx(
                        out=acc[:, si, :],
                        lhsT=codes[:, P * gl : P * (gl + 1)].bitcast(FP8X4),
                        lhsT_scale=scl[:, P * gl : P * (gl + 1)],
                        rhs=act_codes[half][:, P * g : P * (g + 1)].bitcast(FP8X4),
                        rhs_scale=act_scales[half][:, P * g : P * (g + 1)],
                        start=(pi == 0),
                        stop=(pi == len(passes) - 1),
                    )
            gate = st[0][0]
            for si, (gt, t) in enumerate(st):
                nc.scalar.activation(
                    out=gate_out[gate][:, t, :],
                    in_=acc[:, si, :],
                    func=(ACT.Sigmoid if gate == "i" else ACT.Tanh),
                    bias=bias[gate][:, t : t + 1],
                    scale=1.0,
                )
            hi = st[-1][1] + 1
            lo = hi - 1 if hi > 2 * PAIRS else hi - 2
            if gate == "g" and (hi > 2 * PAIRS or hi % 2 == 0):
                nc.vector.tensor_tensor(
                    out=osb[:, lo:hi, :], in0=gate_out["i"][:, lo:hi, :], in1=gate_out["g"][:, lo:hi, :], op=ALU.mult
                )
                if hi == 2 * PAIRS:
                    nc.sync.dma_start(out=out_v[:, 0:hi, :], in_=osb[:, 0:hi, :])
                elif hi > 2 * PAIRS:
                    nc.sync.dma_start(out=out_v[:, lo:hi, :], in_=osb[:, lo:hi, :])

        bank_count = 0
        for ci in range(n_steps):
            if ci == HEAD_STEPS:
                prepare_activations()
            gate, half, t0, n, g0, ng = stream[ci]
            words = raw_tiles[ci][:].bitcast(F32)
            banks = []
            for j in range(n):
                banks.append(transposes(words[:, j * 256 * ng : (j + 1) * 256 * ng], ng))
            if ci + NB < n_steps:
                load(ci + NB)
            grps = []
            for j in range(n):
                grp = grpp.tile([P, K], BF16, name="grp", tag="grp", align_bytes=64)
                grps.append(grp)
                for b, tb in enumerate(banks[j]):
                    bank_count += 1
                    copy_bank("v" if (ng == 4 and bank_count % 4 == 0) else "s", grp, b, tb)
            for j in range(n):
                codes = codp.tile([P, 512], U32, name="codes", tag="codes", align_bytes=64)
                scl = codp.tile([P, 512], U8, name="scl", tag="scl", align_bytes=64)
                quantise(grps[j], codes, scl, ng)
                unit_codes[(ci, j)] = (codes, scl)
            for st in runs.get(ci, []):
                mx_set(st)
